import numpy as np
import ml_dtypes


def mxq(x, axis, fmt="e4m3"):
    dtype, down = {"e4m3": (ml_dtypes.float8_e4m3fn, 7), "e5m2": (ml_dtypes.float8_e5m2, 14)}[fmt]
    v = np.moveaxis(np.asarray(x, np.float32).astype(ml_dtypes.bfloat16).astype(np.float64), axis, -1)
    blocks = v.reshape(v.shape[:-1] + (-1, 32))
    amax = np.abs(blocks).max(-1, keepdims=True)
    byte = np.maximum(np.where(amax > 0, np.frexp(amax)[1] - 1 + 127, 0) - down, 1)
    scale = np.exp2(byte - 127.0)
    codes = (blocks / scale).astype(np.float32).astype(dtype).astype(np.float64)
    return np.moveaxis((codes * scale).reshape(v.shape), -1, axis)


WIDE = False


def mx_kscale(k, group=512):
    if not WIDE:
        return np.ones(k)
    levels = np.array([10, -10, 5, -5, 0])
    if group != 512:
        return np.exp2(np.random.permutation(np.resize(levels, k // group))).repeat(group)
    if k % 512:
        return np.exp2(np.random.permutation(np.resize(levels, k // 32))).repeat(32)
    a = np.empty((k // 512, 16))
    for p in range(k // 512):
        a[p, :8] = np.random.permutation(np.resize(levels, 8))
        for g in range(8):
            far = levels[np.abs(levels - a[p, g]) >= 10]
            a[p, g + 8] = far[np.random.randint(len(far))]
    return np.exp2(a.ravel()).repeat(32)


BF16 = ml_dtypes.bfloat16


def bf(x):
    return np.asarray(x, np.float32).astype(BF16)


def f64(x):
    return np.asarray(x).astype(np.float64)


B, T, D, F = 2, 32, 8192, 4096
TRIPLES = [(1, 2, 3), (1, 4, 5), (1, 7, 6), (2, 4, 6), (2, 5, 7), (3, 4, 7), (3, 6, 5)]
O = len(TRIPLES) + 1
D8, F8 = D // O, F // O


def oct_table():
    tab = [[None] * O for _ in range(O)]
    tab[0][0] = (0, 1.0)
    for i in range(1, O):
        tab[i][i] = (0, 1.0)
        tab[0][i] = (i, 1.0)
        tab[i][0] = (i, -1.0)
    for a, b, c in TRIPLES:
        for p, q, r in ((a, b, c), (b, c, a), (c, a, b)):
            tab[q][r] = (p, 1.0)
            tab[p][r] = (q, -1.0)
    return tab


def oct_linear(xq, w):
    tab = oct_table()
    p = (xq @ mxq(w.reshape(F, D8).T, 0, "e4m3")).reshape(B, T, O, O, F8)
    return np.concatenate([sum(tab[i][k][1] * p[:, :, i, tab[i][k][0]] for i in range(O)) for k in range(O)], axis=2)


def silu(v):
    return v / (1.0 + np.exp(-v))


def setup_inputs():
    s8 = mx_kscale(D8, D8 // 2)
    return {"x": bf(np.random.standard_normal((B, T, D)) * np.tile(s8, O)),
            "wq_gate": bf(np.random.standard_normal((O, F8, D8)) / np.sqrt(D) / s8),
            "wq_up": bf(np.random.standard_normal((O, F8, D8)) / np.sqrt(D) / s8)}


def reference(x, wq_gate, wq_up):
    xq = mxq(f64(x).reshape(B, T, O, D8), 3, "e4m3")
    gate = oct_linear(xq, f64(wq_gate))
    up = oct_linear(xq, f64(wq_up))
    return silu(gate) * up

@@ -1,0 +1,205 @@
+from contextlib import ExitStack
+
+import concourse.mybir as mybir
+from concourse.masks import make_identity
+
+F32 = mybir.dt.float32
+BF16 = mybir.dt.bfloat16
+U32 = mybir.dt.uint32
+U8 = mybir.dt.uint8
+FP8X4 = mybir.dt.float8_e4m3fn_x4
+
+P = 128
+PACK = 4
+K_PASS = P * PACK
+TRIPLES = [(1, 2, 3), (1, 4, 5), (1, 7, 6), (2, 4, 6), (2, 5, 7), (3, 4, 7), (3, 6, 5)]
+O = 8
+ROWS = 64
+D8 = 1024
+F8 = 512
+PASSES = D8 // K_PASS
+PAIRS = O // 2
+CHUNKS = F8 // P
+WORD_BLOCKS = D8 // 2 // P
+BLOCKS_AHEAD = 8
+RUN = 1
+
+FLOPS = 2 * 2 * ROWS * O * O * F8 * D8
+
+
+def octonion_sources():
+    source = {(0, 0): (0, 1.0)}
+    for i in range(1, O):
+        source[(0, i)] = (i, 1.0)
+        source[(i, i)] = (0, 1.0)
+        source[(i, 0)] = (i, -1.0)
+    for a, b, c in TRIPLES:
+        for p, q, r in ((a, b, c), (b, c, a), (c, a, b)):
+            source[(p, r)] = (q, 1.0)
+            source[(q, r)] = (p, -1.0)
+    return source
+
+
+def tile_swiglumlp_pa_kernel(tc, x, wq_gate, wq_up, out):
+    nc = tc.nc
+    source = octonion_sources()
+
+    x_halves = x.rearrange("b t (h f) -> (b t h) f", h=2)
+    blocks = [[x_halves[:, l * D8 : (l + 1) * D8] for l in range(CHUNKS)]]
+    for w in (wq_gate, wq_up):
+        for j in range(O):
+            blocks.append([w[j, c * P : (c + 1) * P, :] for c in range(CHUNKS)])
+    out_parts = out.rearrange("b t (k o) -> k (b t) o", o=F8)
+
+    with ExitStack() as ctx:
+        keep = ctx.enter_context(tc.tile_pool(name="keep", bufs=1))
+        raw_pool = ctx.enter_context(tc.tile_pool(name="raw", bufs=BLOCKS_AHEAD * CHUNKS))
+        grouped_pool = ctx.enter_context(tc.tile_pool(name="grouped", bufs=2))
+        w_mx_pool = ctx.enter_context(tc.tile_pool(name="w_mx", bufs=RUN + 1))
+        result_pool = ctx.enter_context(tc.tile_pool(name="result", bufs=PAIRS))
+        flipped_pool = ctx.enter_context(tc.psum_pool(name="flipped", bufs=4))
+        acc_pool = ctx.enter_context(tc.psum_pool(name="acc", bufs=1))
+        ctx.enter_context(tc.manual_schedule())
+
+        raw = {}
+
+        def load_block(b):
+            raw[b] = []
+            for c in range(CHUNKS):
+                chunk = raw_pool.tile([P, D8], BF16, name="chunk")
+                nc.sync.dma_start(out=chunk[:], in_=blocks[b][c])
+                raw[b].append(chunk)
+
+        for b in range(BLOCKS_AHEAD):
+            load_block(b)
+
+        identity = keep.tile([P, P], F32, name="identity")
+        make_identity(nc, identity[:])
+
+        warm = keep.tile([P, 1], F32, name="warm")
+        nc.vector.memset(warm[:], 0.0)
+        nc.scalar.activation(out=warm[:], in_=warm[:], func=mybir.ActivationFunctionType.Silu)
+
+        def transpose_chunk(b, c):
+            words = raw[b][c][:].bitcast(F32)
+            flipped = flipped_pool.tile([P, WORD_BLOCKS, P], F32, name="flipped")
+            for s in range(WORD_BLOCKS):
+                g, u = divmod(s, 2)
+                every_2nd = words[:, 2 * P * g + u : 2 * P * (g + 1) : 2]
+                nc.tensor.transpose(flipped[:, s, :], every_2nd, identity[:])
+            return flipped
+
+        x_signed = keep.tile([P, 2, O, PASSES, ROWS * PACK], BF16, name="x_signed", align_bytes=64)
+        for l in range(CHUNKS):
+            flipped = transpose_chunk(0, l)
+            by_half = flipped[:].rearrange("p (g u) (r h) -> p h g r u", u=2, h=2)
+            for h in range(2):
+                words_out = x_signed[:, 0, 4 * h + l].bitcast(F32).rearrange(
+                    "p g (r u) -> p g r u", u=2
+                )
+                if l % 2 == 0:
+                    nc.vector.tensor_copy(out=words_out, in_=by_half[:, h])
+                else:
+                    nc.scalar.copy(out=words_out, in_=by_half[:, h])
+        load_block(BLOCKS_AHEAD)
+
+        x_codes = [
+            keep.tile([P, PAIRS, PASSES, P], U32, name="x_codes%d" % j, align_bytes=64)
+            for j in range(O)
+        ]
+        x_scales = [
+            keep.tile([P, PAIRS, PASSES, P], U8, name="x_scales%d" % j, align_bytes=64)
+            for j in range(O)
+        ]
+
+        def quantise_x_for(j):
+            for pair in range(PAIRS):
+                for half in range(2):
+                    i, sign = source[(j, 2 * pair + half)]
+                    columns = slice(half * ROWS, (half + 1) * ROWS)
+                    for g in range(PASSES):
+                        nc.vector.quantize_mx(
+                            out=x_codes[j][:, pair, g, columns].bitcast(FP8X4),
+                            scales=x_scales[j][:, pair, g, columns],
+                            in_=x_signed[:, 0 if sign > 0 else 1, i, g, :],
+                        )
+
+        w_mx = {}
+
+        def prepare_w(n):
+            grouped = grouped_pool.tile([P, PASSES, F8 * PACK], BF16, name="grouped", align_bytes=64)
+            grouped_words = grouped[:].bitcast(F32).rearrange("p g (o u) -> p g o u", u=2)
+            for c in range(CHUNKS):
+                flipped = transpose_chunk(n + 1, c)
+                copy_out = nc.vector.tensor_copy if c == CHUNKS - 1 else nc.scalar.copy
+                copy_out(
+                    out=grouped_words[:, :, c * P : (c + 1) * P, :],
+                    in_=flipped[:].rearrange("p (g u) o -> p g o u", u=2),
+                )
+            if n + 1 + BLOCKS_AHEAD < len(blocks):
+                load_block(n + 1 + BLOCKS_AHEAD)
+            codes = w_mx_pool.tile([P, PASSES, F8], U32, name="w_codes", align_bytes=64)
+            scales = w_mx_pool.tile([P, PASSES, F8], U8, name="w_scales", align_bytes=64)
+            nc.vector.quantize_mx(
+                out=codes[:].rearrange("p g o -> p (g o)").bitcast(FP8X4),
+                scales=scales[:].rearrange("p g o -> p (g o)"),
+                in_=grouped[:].rearrange("p g c -> p (g c)"),
+            )
+            w_mx[n] = (codes, scales)
+
+        acc = {}
+        gate_act = {}
+
+        def multiply(n):
+            j = n % O
+            codes, scales = w_mx[n]
+            for pair in range(PAIRS):
+                if j == 0:
+                    acc[pair] = acc_pool.tile([P, F8], F32, name="acc%d" % pair)
+                for g in range(PASSES):
+                    nc.tensor.matmul_mx(
+                        out=acc[pair][:],
+                        lhsT=x_codes[j][:, pair, g, :].bitcast(FP8X4),
+                        lhsT_scale=x_scales[j][:, pair, g, :],
+                        rhs=codes[:, g, :].bitcast(FP8X4),
+                        rhs_scale=scales[:, g, :],
+                        start=(j == 0 and g == 0),
+                        stop=(j == O - 1 and g == PASSES - 1),
+                    )
+                if n == O - 1:
+                    gate_act[pair] = keep.tile([P, F8], F32, name="gate_act%d" % pair)
+                    nc.scalar.activation(
+                        out=gate_act[pair][:],
+                        in_=acc[pair][:],
+                        func=mybir.ActivationFunctionType.Silu,
+                    )
+                if n == 2 * O - 1:
+                    result = result_pool.tile([P, F8], F32, name="result")
+                    nc.vector.tensor_tensor(
+                        out=result[:], in0=acc[pair][:], in1=gate_act[pair][:], op=mybir.AluOpType.mult
+                    )
+                    for half in range(2):
+                        nc.sync.dma_start(
+                            out=out_parts[2 * pair + half],
+                            in_=result[half * ROWS : (half + 1) * ROWS, :],
+                        )
+
+        quantise_x_for(0)
+        prepare_w(0)
+        nc.vector.tensor_scalar(
+            out=x_signed[:, 1].rearrange("p i g c -> p (i g c)"),
+            in0=x_signed[:, 0].rearrange("p i g c -> p (i g c)"),
+            scalar1=-1.0,
+            scalar2=None,
+            op0=mybir.AluOpType.mult,
+        )
+        for n in range(1, RUN):
+            quantise_x_for(n)
+            prepare_w(n)
+        for n in range(2 * O):
+            if n % RUN == RUN - 1:
+                for ahead in range(n + 1, min(n + 1 + RUN, 2 * O)):
+                    if ahead < O:
+                        quantise_x_for(ahead)
+                    prepare_w(ahead)
+            multiply(n)

@@ -20,9 +20,9 @@ F8 = 512
 PASSES = D8 // K_PASS
 PAIRS = O // 2
 CHUNKS = F8 // P
-WORD_BLOCKS = D8 // 2 // P
+SETS = 2 * PASSES
+RUN_LENGTH = 16
 BLOCKS_AHEAD = 8
-RUN = 1
 
 FLOPS = 2 * 2 * ROWS * O * O * F8 * D8
 
@@ -53,9 +53,10 @@ def tile_swiglumlp_pa_kernel(tc, x, wq_gate, wq_up, out):
 
     with ExitStack() as ctx:
         keep = ctx.enter_context(tc.tile_pool(name="keep", bufs=1))
-        raw_pool = ctx.enter_context(tc.tile_pool(name="raw", bufs=BLOCKS_AHEAD * CHUNKS))
+        raw_pool = ctx.enter_context(tc.tile_pool(name="raw", bufs=BLOCKS_AHEAD))
+        ordered_pool = ctx.enter_context(tc.tile_pool(name="ordered", bufs=3))
         grouped_pool = ctx.enter_context(tc.tile_pool(name="grouped", bufs=2))
-        w_mx_pool = ctx.enter_context(tc.tile_pool(name="w_mx", bufs=RUN + 1))
+        w_mx_pool = ctx.enter_context(tc.tile_pool(name="w_mx", bufs=2))
         result_pool = ctx.enter_context(tc.tile_pool(name="result", bufs=PAIRS))
         flipped_pool = ctx.enter_context(tc.psum_pool(name="flipped", bufs=4))
         acc_pool = ctx.enter_context(tc.psum_pool(name="acc", bufs=1))
@@ -64,11 +65,9 @@ def tile_swiglumlp_pa_kernel(tc, x, wq_gate, wq_up, out):
         raw = {}
 
         def load_block(b):
-            raw[b] = []
+            raw[b] = raw_pool.tile([P, CHUNKS * D8], BF16, name="block")
             for c in range(CHUNKS):
-                chunk = raw_pool.tile([P, D8], BF16, name="chunk")
-                nc.sync.dma_start(out=chunk[:], in_=blocks[b][c])
-                raw[b].append(chunk)
+                nc.sync.dma_start(out=raw[b][:, c * D8 : (c + 1) * D8], in_=blocks[b][c])
 
         for b in range(BLOCKS_AHEAD):
             load_block(b)
@@ -80,16 +79,29 @@ def tile_swiglumlp_pa_kernel(tc, x, wq_gate, wq_up, out):
         nc.vector.memset(warm[:], 0.0)
         nc.scalar.activation(out=warm[:], in_=warm[:], func=mybir.ActivationFunctionType.Silu)
 
+        ordered = {}
+
+        def reorder(b, first, last, copy):
+            if first == 0:
+                ordered[b] = ordered_pool.tile([P, SETS, CHUNKS * D8 // SETS], BF16, name="ordered")
+            columns = slice(first * D8 // SETS, last * D8 // SETS)
+            copy(
+                out=ordered[b][:, :, columns].rearrange("p s (q v) -> p s q v", v=RUN_LENGTH),
+                in_=raw[b][:, first * D8 : last * D8].rearrange(
+                    "p (q s v) -> p s q v", s=SETS, v=RUN_LENGTH
+                ),
+            )
+
         def transpose_chunk(b, c):
-            words = raw[b][c][:].bitcast(F32)
-            flipped = flipped_pool.tile([P, WORD_BLOCKS, P], F32, name="flipped")
-            for s in range(WORD_BLOCKS):
-                g, u = divmod(s, 2)
-                every_2nd = words[:, 2 * P * g + u : 2 * P * (g + 1) : 2]
-                nc.tensor.transpose(flipped[:, s, :], every_2nd, identity[:])
+            flipped = flipped_pool.tile([P, SETS, P], F32, name="flipped")
+            for s in range(SETS):
+                pairs = ordered[b][:, s, 2 * P * c : 2 * P * (c + 1)].bitcast(F32)
+                nc.tensor.transpose(flipped[:, s, :], pairs, identity[:])
             return flipped
 
         x_signed = keep.tile([P, 2, O, PASSES, ROWS * PACK], BF16, name="x_signed", align_bytes=64)
+        for l in range(CHUNKS):
+            reorder(0, l, l + 1, nc.vector.tensor_copy)
         for l in range(CHUNKS):
             flipped = transpose_chunk(0, l)
             by_half = flipped[:].rearrange("p (g u) (r h) -> p h g r u", u=2, h=2)
@@ -102,6 +114,8 @@ def tile_swiglumlp_pa_kernel(tc, x, wq_gate, wq_up, out):
                 else:
                     nc.scalar.copy(out=words_out, in_=by_half[:, h])
         load_block(BLOCKS_AHEAD)
+        for c in range(CHUNKS):
+            reorder(1, c, c + 1, nc.vector.tensor_copy if c % 2 == 0 else nc.scalar.copy)
 
         x_codes = [
             keep.tile([P, PAIRS, PASSES, P], U32, name="x_codes%d" % j, align_bytes=64)
@@ -136,8 +150,6 @@ def tile_swiglumlp_pa_kernel(tc, x, wq_gate, wq_up, out):
                     out=grouped_words[:, :, c * P : (c + 1) * P, :],
                     in_=flipped[:].rearrange("p (g u) o -> p g o u", u=2),
                 )
-            if n + 1 + BLOCKS_AHEAD < len(blocks):
-                load_block(n + 1 + BLOCKS_AHEAD)
             codes = w_mx_pool.tile([P, PASSES, F8], U32, name="w_codes", align_bytes=64)
             scales = w_mx_pool.tile([P, PASSES, F8], U8, name="w_scales", align_bytes=64)
             nc.vector.quantize_mx(
@@ -186,6 +198,9 @@ def tile_swiglumlp_pa_kernel(tc, x, wq_gate, wq_up, out):
 
         quantise_x_for(0)
         prepare_w(0)
+        reorder(2, 0, CHUNKS, nc.vector.tensor_copy)
+        for b in (1, 2):
+            load_block(b + BLOCKS_AHEAD)
         nc.vector.tensor_scalar(
             out=x_signed[:, 1].rearrange("p i g c -> p (i g c)"),
             in0=x_signed[:, 0].rearrange("p i g c -> p (i g c)"),
@@ -193,13 +208,13 @@ def tile_swiglumlp_pa_kernel(tc, x, wq_gate, wq_up, out):
             scalar2=None,
             op0=mybir.AluOpType.mult,
         )
-        for n in range(1, RUN):
-            quantise_x_for(n)
-            prepare_w(n)
         for n in range(2 * O):
-            if n % RUN == RUN - 1:
-                for ahead in range(n + 1, min(n + 1 + RUN, 2 * O)):
-                    if ahead < O:
-                        quantise_x_for(ahead)
-                    prepare_w(ahead)
+            if n + 3 < len(blocks):
+                reorder(n + 3, 0, CHUNKS, nc.vector.tensor_copy)
+                if n + 3 + BLOCKS_AHEAD < len(blocks):
+                    load_block(n + 3 + BLOCKS_AHEAD)
+            if n + 1 < 2 * O:
+                if n + 1 < O:
+                    quantise_x_for(n + 1)
+                prepare_w(n + 1)
             multiply(n)

@@ -40,9 +40,39 @@ def octonion_sources():
     return source
 
 
+def place_components(source):
+    wanted = {}
+    for j in range(O):
+        for pair in range(PAIRS):
+            wanted[(j, pair)] = (source[(j, 2 * pair)], source[(j, 2 * pair + 1)])
+    left = []
+    for two in wanted.values():
+        if two not in left:
+            left.append(two)
+    slots, place = [], {}
+    while left:
+        chain = list(left[0])
+        left = left[1:]
+        growing = True
+        while growing:
+            behind = [two for two in left if two[0] == chain[-1]]
+            before = [two for two in left if two[1] == chain[0]]
+            growing = bool(behind or before)
+            if behind:
+                chain = chain + [behind[0][1]]
+                left.remove(behind[0])
+            elif before:
+                chain = [before[0][0]] + chain
+                left.remove(before[0])
+        for a in range(len(chain) - 1):
+            place[(chain[a], chain[a + 1])] = len(slots) + a
+        slots = slots + chain
+    return slots, {key: place[two] for key, two in wanted.items()}
+
+
 def tile_swiglumlp_pa_kernel(tc, x, wq_gate, wq_up, out):
     nc = tc.nc
-    source = octonion_sources()
+    slots, first_slot = place_components(octonion_sources())
 
     x_halves = x.rearrange("b t (h f) -> (b t h) f", h=2)
     blocks = [[x_halves[:, l * D8 : (l + 1) * D8] for l in range(CHUNKS)]]
@@ -99,48 +129,45 @@ def tile_swiglumlp_pa_kernel(tc, x, wq_gate, wq_up, out):
                 nc.tensor.transpose(flipped[:, s, :], pairs, identity[:])
             return flipped
 
-        x_signed = keep.tile([P, 2, O, PASSES, ROWS * PACK], BF16, name="x_signed", align_bytes=64)
+        x_signed = keep.tile([P, 2, PASSES, O, ROWS * PACK], BF16, name="x_signed", align_bytes=64)
         for l in range(CHUNKS):
             reorder(0, l, l + 1, nc.vector.tensor_copy)
         for l in range(CHUNKS):
             flipped = transpose_chunk(0, l)
             by_half = flipped[:].rearrange("p (g u) (r h) -> p h g r u", u=2, h=2)
             for h in range(2):
-                words_out = x_signed[:, 0, 4 * h + l].bitcast(F32).rearrange(
+                words_out = x_signed[:, 0, :, 4 * h + l].bitcast(F32).rearrange(
                     "p g (r u) -> p g r u", u=2
                 )
                 if l % 2 == 0:
                     nc.vector.tensor_copy(out=words_out, in_=by_half[:, h])
                 else:
                     nc.scalar.copy(out=words_out, in_=by_half[:, h])
+            reorder(1, l, l + 1, nc.vector.tensor_copy)
         load_block(BLOCKS_AHEAD)
-        for c in range(CHUNKS):
-            reorder(1, c, c + 1, nc.vector.tensor_copy if c % 2 == 0 else nc.scalar.copy)
 
-        x_codes = [
-            keep.tile([P, PAIRS, PASSES, P], U32, name="x_codes%d" % j, align_bytes=64)
-            for j in range(O)
-        ]
-        x_scales = [
-            keep.tile([P, PAIRS, PASSES, P], U8, name="x_scales%d" % j, align_bytes=64)
-            for j in range(O)
-        ]
+        x_codes = keep.tile([P, PASSES, len(slots) * ROWS], U32, name="x_codes", align_bytes=64)
+        x_scales = keep.tile([P, PASSES, len(slots) * ROWS], U8, name="x_scales", align_bytes=64)
+        filled = []
 
         def quantise_x_for(j):
             for pair in range(PAIRS):
-                for half in range(2):
-                    i, sign = source[(j, 2 * pair + half)]
-                    columns = slice(half * ROWS, (half + 1) * ROWS)
+                for slot in range(first_slot[(j, pair)], first_slot[(j, pair)] + 2):
+                    if slot in filled:
+                        continue
+                    filled.append(slot)
+                    i, sign = slots[slot]
+                    columns = slice(slot * ROWS, (slot + 1) * ROWS)
                     for g in range(PASSES):
                         nc.vector.quantize_mx(
-                            out=x_codes[j][:, pair, g, columns].bitcast(FP8X4),
-                            scales=x_scales[j][:, pair, g, columns],
-                            in_=x_signed[:, 0 if sign > 0 else 1, i, g, :],
+                            out=x_codes[:, g, columns].bitcast(FP8X4),
+                            scales=x_scales[:, g, columns],
+                            in_=x_signed[:, 0 if sign > 0 else 1, g, i, :],
                         )
 
         w_mx = {}
 
-        def prepare_w(n):
+        def transpose_w(n):
             grouped = grouped_pool.tile([P, PASSES, F8 * PACK], BF16, name="grouped", align_bytes=64)
             grouped_words = grouped[:].bitcast(F32).rearrange("p g (o u) -> p g o u", u=2)
             for c in range(CHUNKS):
@@ -150,6 +177,9 @@ def tile_swiglumlp_pa_kernel(tc, x, wq_gate, wq_up, out):
                     out=grouped_words[:, :, c * P : (c + 1) * P, :],
                     in_=flipped[:].rearrange("p (g u) o -> p g o u", u=2),
                 )
+            return grouped
+
+        def quantise_w(n, grouped):
             codes = w_mx_pool.tile([P, PASSES, F8], U32, name="w_codes", align_bytes=64)
             scales = w_mx_pool.tile([P, PASSES, F8], U8, name="w_scales", align_bytes=64)
             nc.vector.quantize_mx(
@@ -168,11 +198,14 @@ def tile_swiglumlp_pa_kernel(tc, x, wq_gate, wq_up, out):
             for pair in range(PAIRS):
                 if j == 0:
                     acc[pair] = acc_pool.tile([P, F8], F32, name="acc%d" % pair)
+                two_slots = slice(
+                    first_slot[(j, pair)] * ROWS, (first_slot[(j, pair)] + 2) * ROWS
+                )
                 for g in range(PASSES):
                     nc.tensor.matmul_mx(
                         out=acc[pair][:],
-                        lhsT=x_codes[j][:, pair, g, :].bitcast(FP8X4),
-                        lhsT_scale=x_scales[j][:, pair, g, :],
+                        lhsT=x_codes[:, g, two_slots].bitcast(FP8X4),
+                        lhsT_scale=x_scales[:, g, two_slots],
                         rhs=codes[:, g, :].bitcast(FP8X4),
                         rhs_scale=scales[:, g, :],
                         start=(j == 0 and g == 0),
@@ -197,13 +230,15 @@ def tile_swiglumlp_pa_kernel(tc, x, wq_gate, wq_up, out):
                         )
 
         quantise_x_for(0)
-        prepare_w(0)
-        reorder(2, 0, CHUNKS, nc.vector.tensor_copy)
+        grouped = transpose_w(0)
+        reorder(2, 0, 2, nc.scalar.copy)
+        reorder(2, 2, CHUNKS, nc.vector.tensor_copy)
+        quantise_w(0, grouped)
         for b in (1, 2):
             load_block(b + BLOCKS_AHEAD)
         nc.vector.tensor_scalar(
-            out=x_signed[:, 1].rearrange("p i g c -> p (i g c)"),
-            in0=x_signed[:, 0].rearrange("p i g c -> p (i g c)"),
+            out=x_signed[:, 1].rearrange("p g i c -> p (g i c)"),
+            in0=x_signed[:, 0].rearrange("p g i c -> p (g i c)"),
             scalar1=-1.0,
             scalar2=None,
             op0=mybir.AluOpType.mult,
@@ -216,5 +251,5 @@ def tile_swiglumlp_pa_kernel(tc, x, wq_gate, wq_up, out):
             if n + 1 < 2 * O:
                 if n + 1 < O:
                     quantise_x_for(n + 1)
-                prepare_w(n + 1)
+                quantise_w(n + 1, transpose_w(n + 1))
             multiply(n)

@@ -113,19 +113,19 @@ def tile_swiglumlp_pa_kernel(tc, x, wq_gate, wq_up, out):
 
         def reorder(b, first, last, copy):
             if first == 0:
-                ordered[b] = ordered_pool.tile([P, SETS, CHUNKS * D8 // SETS], BF16, name="ordered")
-            columns = slice(first * D8 // SETS, last * D8 // SETS)
+                ordered[b] = ordered_pool.tile([P, CHUNKS * D8], BF16, name="ordered")
+            columns = slice(first * D8, last * D8)
+            sizes = {"c": last - first, "s": SETS, "v": RUN_LENGTH}
             copy(
-                out=ordered[b][:, :, columns].rearrange("p s (q v) -> p s q v", v=RUN_LENGTH),
-                in_=raw[b][:, first * D8 : last * D8].rearrange(
-                    "p (q s v) -> p s q v", s=SETS, v=RUN_LENGTH
-                ),
+                out=ordered[b][:, columns].rearrange("p (c s q v) -> p c s q v", **sizes),
+                in_=raw[b][:, columns].rearrange("p (c q s v) -> p c s q v", **sizes),
             )
 
         def transpose_chunk(b, c):
             flipped = flipped_pool.tile([P, SETS, P], F32, name="flipped")
             for s in range(SETS):
-                pairs = ordered[b][:, s, 2 * P * c : 2 * P * (c + 1)].bitcast(F32)
+                start = c * D8 + s * 2 * P
+                pairs = ordered[b][:, start : start + 2 * P].bitcast(F32)
                 nc.tensor.transpose(flipped[:, s, :], pairs, identity[:])
             return flipped
 
@@ -172,7 +172,7 @@ def tile_swiglumlp_pa_kernel(tc, x, wq_gate, wq_up, out):
             grouped_words = grouped[:].bitcast(F32).rearrange("p g (o u) -> p g o u", u=2)
             for c in range(CHUNKS):
                 flipped = transpose_chunk(n + 1, c)
-                copy_out = nc.vector.tensor_copy if c == CHUNKS - 1 else nc.scalar.copy
+                copy_out = nc.vector.tensor_copy if n > 0 and c == CHUNKS - 1 else nc.scalar.copy
                 copy_out(
                     out=grouped_words[:, :, c * P : (c + 1) * P, :],
                     in_=flipped[:].rearrange("p (g u) o -> p g o u", u=2),
@@ -230,10 +230,11 @@ def tile_swiglumlp_pa_kernel(tc, x, wq_gate, wq_up, out):
                         )
 
         quantise_x_for(0)
-        grouped = transpose_w(0)
-        reorder(2, 0, 2, nc.scalar.copy)
-        reorder(2, 2, CHUNKS, nc.vector.tensor_copy)
-        quantise_w(0, grouped)
+        quantise_w(0, transpose_w(0))
+        for c in (0, 1):
+            reorder(2, c, c + 1, nc.scalar.copy)
+        for c in (2, 3):
+            reorder(2, c, c + 1, nc.vector.tensor_copy)
         for b in (1, 2):
             load_block(b + BLOCKS_AHEAD)
         nc.vector.tensor_scalar(

@@ -22,6 +22,9 @@ PAIRS = O // 2
 CHUNKS = F8 // P
 SETS = 2 * PASSES
 RUN_LENGTH = 16
+WARM_START = 6
+WARM_AFTER_X = 3
+WARM_AFTER_FIRST = 4
 BLOCKS_AHEAD = 8
 
 FLOPS = 2 * 2 * ROWS * O * O * F8 * D8
@@ -109,6 +112,18 @@ def tile_swiglumlp_pa_kernel(tc, x, wq_gate, wq_up, out):
         nc.vector.memset(warm[:], 0.0)
         nc.scalar.activation(out=warm[:], in_=warm[:], func=mybir.ActivationFunctionType.Silu)
 
+        zeros = keep.tile([P, F8], BF16, name="zeros")
+        nc.vector.memset(zeros[:], 0.0)
+        zero_sums = acc_pool.tile([P, F8], F32, name="acc%d" % (PAIRS - 1))
+
+        def keep_warm(count):
+            for turn in range(count):
+                nc.tensor.matmul(
+                    zero_sums[:], lhsT=zeros[:, :P], rhs=zeros[:], start=True, stop=True
+                )
+
+        keep_warm(WARM_START)
+
         ordered = {}
 
         def reorder(b, first, last, copy):
@@ -145,6 +160,8 @@ def tile_swiglumlp_pa_kernel(tc, x, wq_gate, wq_up, out):
                     nc.scalar.copy(out=words_out, in_=by_half[:, h])
             reorder(1, l, l + 1, nc.vector.tensor_copy)
         load_block(BLOCKS_AHEAD)
+
+        keep_warm(WARM_AFTER_X)
 
         x_codes = keep.tile([P, PASSES, len(slots) * ROWS], U32, name="x_codes", align_bytes=64)
         x_scales = keep.tile([P, PASSES, len(slots) * ROWS], U8, name="x_scales", align_bytes=64)
@@ -231,6 +248,7 @@ def tile_swiglumlp_pa_kernel(tc, x, wq_gate, wq_up, out):
 
         quantise_x_for(0)
         quantise_w(0, transpose_w(0))
+        keep_warm(WARM_AFTER_FIRST)
         for c in (0, 1):
             reorder(2, c, c + 1, nc.scalar.copy)
         for c in (2, 3):

@@ -30,6 +30,17 @@ BLOCKS_AHEAD = 8
 FLOPS = 2 * 2 * ROWS * O * O * F8 * D8
 
 
+X = -1
+BY_VECTOR = (13, 14, 15)
+QUADRANTS = 4
+QUADRANT = P // QUADRANTS
+PIECE = D8 // QUADRANTS
+
+
+def reorder_turn(n):
+    return 4 + 3 * BY_VECTOR.index(n) if n in BY_VECTOR else n - 2
+
+
 def octonion_sources():
     source = {(0, 0): (0, 1.0)}
     for i in range(1, O):
@@ -78,18 +89,18 @@ def tile_swiglumlp_pa_kernel(tc, x, wq_gate, wq_up, out):
     slots, first_slot = place_components(octonion_sources())
 
     x_halves = x.rearrange("b t (h f) -> (b t h) f", h=2)
-    blocks = [[x_halves[:, l * D8 : (l + 1) * D8] for l in range(CHUNKS)]]
-    for w in (wq_gate, wq_up):
-        for j in range(O):
-            blocks.append([w[j, c * P : (c + 1) * P, :] for c in range(CHUNKS)])
+    matrices = [w[j] for w in (wq_gate, wq_up) for j in range(O)]
+    load_order = [X] + sorted(range(2 * O), key=lambda n: (reorder_turn(n), n not in BY_VECTOR))
     out_parts = out.rearrange("b t (k o) -> k (b t) o", o=F8)
 
     with ExitStack() as ctx:
         keep = ctx.enter_context(tc.tile_pool(name="keep", bufs=1))
         raw_pool = ctx.enter_context(tc.tile_pool(name="raw", bufs=BLOCKS_AHEAD))
-        ordered_pool = ctx.enter_context(tc.tile_pool(name="ordered", bufs=3))
-        grouped_pool = ctx.enter_context(tc.tile_pool(name="grouped", bufs=2))
-        w_mx_pool = ctx.enter_context(tc.tile_pool(name="w_mx", bufs=2))
+        ordered_pool = ctx.enter_context(tc.tile_pool(name="ordered", bufs=4))
+        turned_pool = ctx.enter_context(tc.tile_pool(name="turned", bufs=1))
+        grouped_pool = ctx.enter_context(tc.tile_pool(name="grouped", bufs=3))
+        next_mx_pool = ctx.enter_context(tc.tile_pool(name="next_mx", bufs=2))
+        early_mx_pool = ctx.enter_context(tc.tile_pool(name="early_mx", bufs=len(BY_VECTOR)))
         result_pool = ctx.enter_context(tc.tile_pool(name="result", bufs=PAIRS))
         flipped_pool = ctx.enter_context(tc.psum_pool(name="flipped", bufs=4))
         acc_pool = ctx.enter_context(tc.psum_pool(name="acc", bufs=1))
@@ -97,13 +108,30 @@ def tile_swiglumlp_pa_kernel(tc, x, wq_gate, wq_up, out):
 
         raw = {}
 
+        reordered = []
+
         def load_block(b):
             raw[b] = raw_pool.tile([P, CHUNKS * D8], BF16, name="block")
+            if b in BY_VECTOR:
+                for m in range(F8 // QUADRANT):
+                    rows = matrices[b][m * QUADRANT : (m + 1) * QUADRANT, :]
+                    nc.sync.dma_start(
+                        out=raw[b][:, m * PIECE : (m + 1) * PIECE],
+                        in_=rows.rearrange("r (q k) -> q r k", q=QUADRANTS),
+                    )
+                return
             for c in range(CHUNKS):
-                nc.sync.dma_start(out=raw[b][:, c * D8 : (c + 1) * D8], in_=blocks[b][c])
+                columns = slice(c * D8, (c + 1) * D8)
+                chunk = x_halves[:, columns] if b == X else matrices[b][c * P : (c + 1) * P, :]
+                nc.sync.dma_start(out=raw[b][:, columns], in_=chunk)
 
-        for b in range(BLOCKS_AHEAD):
-            load_block(b)
+        def load_more():
+            while len(raw) < len(load_order) and (
+                len(raw) < BLOCKS_AHEAD or load_order[len(raw) - BLOCKS_AHEAD] in reordered
+            ):
+                load_block(load_order[len(raw)])
+
+        load_more()
 
         identity = keep.tile([P, P], F32, name="identity")
         make_identity(nc, identity[:])
@@ -126,15 +154,27 @@ def tile_swiglumlp_pa_kernel(tc, x, wq_gate, wq_up, out):
 
         ordered = {}
 
-        def reorder(b, first, last, copy):
+        def reorder(b, first, last, copy, dtype=BF16):
             if first == 0:
-                ordered[b] = ordered_pool.tile([P, CHUNKS * D8], BF16, name="ordered")
+                ordered[b] = ordered_pool.tile(
+                    [P, CHUNKS * D8], BF16, name="ordered", align_bytes=64
+                )
             columns = slice(first * D8, last * D8)
-            sizes = {"c": last - first, "s": SETS, "v": RUN_LENGTH}
+            length = PIECE if b in BY_VECTOR else D8
+            sizes = {
+                "c": (last - first) * D8 // length,
+                "s": SETS,
+                "v": RUN_LENGTH if dtype == BF16 else RUN_LENGTH // 2,
+            }
+            out_view = ordered[b][:, columns].bitcast(dtype)
+            in_view = raw[b][:, columns].bitcast(dtype)
             copy(
-                out=ordered[b][:, columns].rearrange("p (c s q v) -> p c s q v", **sizes),
-                in_=raw[b][:, columns].rearrange("p (c q s v) -> p c s q v", **sizes),
+                out=out_view.rearrange("p (c s q v) -> p c s q v", **sizes),
+                in_=in_view.rearrange("p (c q s v) -> p c s q v", **sizes),
             )
+            if last == CHUNKS:
+                reordered.append(b)
+                load_more()
 
         def transpose_chunk(b, c):
             flipped = flipped_pool.tile([P, SETS, P], F32, name="flipped")
@@ -146,9 +186,9 @@ def tile_swiglumlp_pa_kernel(tc, x, wq_gate, wq_up, out):
 
         x_signed = keep.tile([P, 2, PASSES, O, ROWS * PACK], BF16, name="x_signed", align_bytes=64)
         for l in range(CHUNKS):
-            reorder(0, l, l + 1, nc.vector.tensor_copy)
+            reorder(X, l, l + 1, nc.vector.tensor_copy)
         for l in range(CHUNKS):
-            flipped = transpose_chunk(0, l)
+            flipped = transpose_chunk(X, l)
             by_half = flipped[:].rearrange("p (g u) (r h) -> p h g r u", u=2, h=2)
             for h in range(2):
                 words_out = x_signed[:, 0, :, 4 * h + l].bitcast(F32).rearrange(
@@ -158,8 +198,7 @@ def tile_swiglumlp_pa_kernel(tc, x, wq_gate, wq_up, out):
                     nc.vector.tensor_copy(out=words_out, in_=by_half[:, h])
                 else:
                     nc.scalar.copy(out=words_out, in_=by_half[:, h])
-            reorder(1, l, l + 1, nc.vector.tensor_copy)
-        load_block(BLOCKS_AHEAD)
+            reorder(0, l, l + 1, nc.vector.tensor_copy)
 
         keep_warm(WARM_AFTER_X)
 
@@ -188,15 +227,37 @@ def tile_swiglumlp_pa_kernel(tc, x, wq_gate, wq_up, out):
             grouped = grouped_pool.tile([P, PASSES, F8 * PACK], BF16, name="grouped", align_bytes=64)
             grouped_words = grouped[:].bitcast(F32).rearrange("p g (o u) -> p g o u", u=2)
             for c in range(CHUNKS):
-                flipped = transpose_chunk(n + 1, c)
-                copy_out = nc.vector.tensor_copy if n > 0 and c == CHUNKS - 1 else nc.scalar.copy
-                copy_out(
+                flipped = transpose_chunk(n, c)
+                nc.scalar.copy(
                     out=grouped_words[:, :, c * P : (c + 1) * P, :],
                     in_=flipped[:].rearrange("p (g u) o -> p g o u", u=2),
                 )
             return grouped
 
+        turned = {}
+
+        def turn_on_vector(n, half):
+            if half == 0:
+                turned[n] = turned_pool.tile([P, CHUNKS * D8 // 2], F32, name="turned", align_bytes=64)
+            columns = slice(half * D8, (half + 1) * D8)
+            nc.vector.transpose(turned[n][:, columns], ordered[n][:].bitcast(F32)[:, columns])
+
+        def group_turned(n):
+            grouped = grouped_pool.tile([P, PASSES, F8 * PACK], BF16, name="grouped", align_bytes=64)
+            by_pass = turned[n][:].rearrange(
+                "p (m g u r) -> p g m r u", g=PASSES, u=2, r=QUADRANT
+            )
+            for g in range(PASSES):
+                nc.scalar.copy(
+                    out=grouped[:, g, :].bitcast(F32).rearrange(
+                        "p (m r u) -> p m r u", r=QUADRANT, u=2
+                    ),
+                    in_=by_pass[:, g],
+                )
+            return grouped
+
         def quantise_w(n, grouped):
+            w_mx_pool = early_mx_pool if n in BY_VECTOR else next_mx_pool
             codes = w_mx_pool.tile([P, PASSES, F8], U32, name="w_codes", align_bytes=64)
             scales = w_mx_pool.tile([P, PASSES, F8], U8, name="w_scales", align_bytes=64)
             nc.vector.quantize_mx(
@@ -250,11 +311,9 @@ def tile_swiglumlp_pa_kernel(tc, x, wq_gate, wq_up, out):
         quantise_w(0, transpose_w(0))
         keep_warm(WARM_AFTER_FIRST)
         for c in (0, 1):
-            reorder(2, c, c + 1, nc.scalar.copy)
+            reorder(1, c, c + 1, nc.scalar.copy, F32)
         for c in (2, 3):
-            reorder(2, c, c + 1, nc.vector.tensor_copy)
-        for b in (1, 2):
-            load_block(b + BLOCKS_AHEAD)
+            reorder(1, c, c + 1, nc.vector.tensor_copy)
         nc.vector.tensor_scalar(
             out=x_signed[:, 1].rearrange("p g i c -> p (g i c)"),
             in0=x_signed[:, 0].rearrange("p g i c -> p (g i c)"),
@@ -262,13 +321,27 @@ def tile_swiglumlp_pa_kernel(tc, x, wq_gate, wq_up, out):
             scalar2=None,
             op0=mybir.AluOpType.mult,
         )
+        grouped = {}
         for n in range(2 * O):
-            if n + 3 < len(blocks):
-                reorder(n + 3, 0, CHUNKS, nc.vector.tensor_copy)
-                if n + 3 + BLOCKS_AHEAD < len(blocks):
-                    load_block(n + 3 + BLOCKS_AHEAD)
-            if n + 1 < 2 * O:
-                if n + 1 < O:
-                    quantise_x_for(n + 1)
-                quantise_w(n + 1, transpose_w(n + 1))
+            by_tensor = n + 1 not in BY_VECTOR and n + 1 < 2 * O
+            for m in range(2 * O):
+                if m not in BY_VECTOR and reorder_turn(m) == n:
+                    reorder(m, 0, CHUNKS, nc.vector.tensor_copy)
+            if n + 1 < O:
+                quantise_x_for(n + 1)
+            if by_tensor:
+                grouped[n + 1] = transpose_w(n + 1)
+            for m in BY_VECTOR:
+                step = n - reorder_turn(m)
+                if step == 0:
+                    reorder(m, 0, CHUNKS, nc.vector.tensor_copy)
+                if step in (1, 2):
+                    turn_on_vector(m, step - 1)
+                if step == 4:
+                    quantise_w(m, grouped[m])
+            if by_tensor:
+                quantise_w(n + 1, grouped[n + 1])
+            for m in BY_VECTOR:
+                if n - reorder_turn(m) == 3:
+                    grouped[m] = group_turned(m)
             multiply(n)

@@ -22,7 +22,7 @@ PAIRS = O // 2
 CHUNKS = F8 // P
 SETS = 2 * PASSES
 RUN_LENGTH = 16
-WARM_START = 6
+WARM_START = 4
 WARM_AFTER_X = 3
 WARM_AFTER_FIRST = 4
 BLOCKS_AHEAD = 8
@@ -31,14 +31,14 @@ FLOPS = 2 * 2 * ROWS * O * O * F8 * D8
 
 
 X = -1
-BY_VECTOR = (13, 14, 15)
+BY_VECTOR = (14, 15)
 QUADRANTS = 4
 QUADRANT = P // QUADRANTS
 PIECE = D8 // QUADRANTS
 
 
 def reorder_turn(n):
-    return 4 + 3 * BY_VECTOR.index(n) if n in BY_VECTOR else n - 2
+    return 7 + 3 * BY_VECTOR.index(n) if n in BY_VECTOR else n - 2
 
 
 def octonion_sources():
@@ -90,7 +90,7 @@ def tile_swiglumlp_pa_kernel(tc, x, wq_gate, wq_up, out):
 
     x_halves = x.rearrange("b t (h f) -> (b t h) f", h=2)
     matrices = [w[j] for w in (wq_gate, wq_up) for j in range(O)]
-    load_order = [X] + sorted(range(2 * O), key=lambda n: (reorder_turn(n), n not in BY_VECTOR))
+    load_order = [X] + sorted(range(2 * O), key=lambda n: (reorder_turn(n), n))
     out_parts = out.rearrange("b t (k o) -> k (b t) o", o=F8)
 
     with ExitStack() as ctx:
@@ -113,12 +113,19 @@ def tile_swiglumlp_pa_kernel(tc, x, wq_gate, wq_up, out):
         def load_block(b):
             raw[b] = raw_pool.tile([P, CHUNKS * D8], BF16, name="block")
             if b in BY_VECTOR:
-                for m in range(F8 // QUADRANT):
-                    rows = matrices[b][m * QUADRANT : (m + 1) * QUADRANT, :]
-                    nc.sync.dma_start(
-                        out=raw[b][:, m * PIECE : (m + 1) * PIECE],
-                        in_=rows.rearrange("r (q k) -> q r k", q=QUADRANTS),
+                for q4 in range(QUADRANTS):
+                    partitions = slice(q4 * QUADRANT, (q4 + 1) * QUADRANT)
+                    quarter = matrices[b][:, q4 * PIECE : (q4 + 1) * PIECE]
+                    nc.gpsimd.dma_start(
+                        out=raw[b][partitions, :].rearrange("r (m k) -> r m k", k=PIECE),
+                        in_=quarter.rearrange("(m r) k -> r m k", r=QUADRANT),
                     )
+                return
+            if b not in (X, 0, 1):
+                nc.sync.dma_start(
+                    out=raw[b][:].rearrange("p (c k) -> p c k", k=D8),
+                    in_=matrices[b].rearrange("(c p) k -> p c k", p=P),
+                )
                 return
             for c in range(CHUNKS):
                 columns = slice(c * D8, (c + 1) * D8)
@@ -155,7 +162,7 @@ def tile_swiglumlp_pa_kernel(tc, x, wq_gate, wq_up, out):
         ordered = {}
 
         def reorder(b, first, last, copy, dtype=BF16):
-            if first == 0:
+            if b not in ordered:
                 ordered[b] = ordered_pool.tile(
                     [P, CHUNKS * D8], BF16, name="ordered", align_bytes=64
                 )
@@ -308,12 +315,12 @@ def tile_swiglumlp_pa_kernel(tc, x, wq_gate, wq_up, out):
                         )
 
         quantise_x_for(0)
-        quantise_w(0, transpose_w(0))
+        first_grouped = transpose_w(0)
+        reorder(1, 0, 1, nc.vector.tensor_copy)
+        quantise_w(0, first_grouped)
         keep_warm(WARM_AFTER_FIRST)
-        for c in (0, 1):
+        for c in range(1, CHUNKS):
             reorder(1, c, c + 1, nc.scalar.copy, F32)
-        for c in (2, 3):
-            reorder(1, c, c + 1, nc.vector.tensor_copy)
         nc.vector.tensor_scalar(
             out=x_signed[:, 1].rearrange("p g i c -> p (g i c)"),
             in0=x_signed[:, 0].rearrange("p g i c -> p (g i c)"),

from contextlib import ExitStack

import concourse.mybir as mybir
from concourse.masks import make_identity

F32 = mybir.dt.float32
BF16 = mybir.dt.bfloat16
U32 = mybir.dt.uint32
U8 = mybir.dt.uint8
FP8X4 = mybir.dt.float8_e4m3fn_x4

P = 128
PACK = 4
K_PASS = P * PACK
TRIPLES = [(1, 2, 3), (1, 4, 5), (1, 7, 6), (2, 4, 6), (2, 5, 7), (3, 4, 7), (3, 6, 5)]
O = 8
ROWS = 64
D8 = 1024
F8 = 512
PASSES = D8 // K_PASS
PAIRS = O // 2
CHUNKS = F8 // P
SETS = 2 * PASSES
RUN_LENGTH = 16
WARM_START = 4
WARM_AFTER_X = 3
WARM_AFTER_FIRST = 4
BLOCKS_AHEAD = 8

FLOPS = 2 * 2 * ROWS * O * O * F8 * D8


X = -1
BY_VECTOR = (14, 15)
QUADRANTS = 4
QUADRANT = P // QUADRANTS
PIECE = D8 // QUADRANTS


def reorder_turn(n):
    return 7 + 3 * BY_VECTOR.index(n) if n in BY_VECTOR else n - 2


def octonion_sources():
    source = {(0, 0): (0, 1.0)}
    for i in range(1, O):
        source[(0, i)] = (i, 1.0)
        source[(i, i)] = (0, 1.0)
        source[(i, 0)] = (i, -1.0)
    for a, b, c in TRIPLES:
        for p, q, r in ((a, b, c), (b, c, a), (c, a, b)):
            source[(p, r)] = (q, 1.0)
            source[(q, r)] = (p, -1.0)
    return source


def place_components(source):
    wanted = {}
    for j in range(O):
        for pair in range(PAIRS):
            wanted[(j, pair)] = (source[(j, 2 * pair)], source[(j, 2 * pair + 1)])
    left = []
    for two in wanted.values():
        if two not in left:
            left.append(two)
    slots, place = [], {}
    while left:
        chain = list(left[0])
        left = left[1:]
        growing = True
        while growing:
            behind = [two for two in left if two[0] == chain[-1]]
            before = [two for two in left if two[1] == chain[0]]
            growing = bool(behind or before)
            if behind:
                chain = chain + [behind[0][1]]
                left.remove(behind[0])
            elif before:
                chain = [before[0][0]] + chain
                left.remove(before[0])
        for a in range(len(chain) - 1):
            place[(chain[a], chain[a + 1])] = len(slots) + a
        slots = slots + chain
    return slots, {key: place[two] for key, two in wanted.items()}


def tile_swiglumlp_pa_kernel(tc, x, wq_gate, wq_up, out):
    nc = tc.nc
    slots, first_slot = place_components(octonion_sources())

    x_halves = x.rearrange("b t (h f) -> (b t h) f", h=2)
    matrices = [w[j] for w in (wq_gate, wq_up) for j in range(O)]
    load_order = [X] + sorted(range(2 * O), key=lambda n: (reorder_turn(n), n))
    out_parts = out.rearrange("b t (k o) -> k (b t) o", o=F8)

    with ExitStack() as ctx:
        keep = ctx.enter_context(tc.tile_pool(name="keep", bufs=1))
        raw_pool = ctx.enter_context(tc.tile_pool(name="raw", bufs=BLOCKS_AHEAD))
        ordered_pool = ctx.enter_context(tc.tile_pool(name="ordered", bufs=4))
        turned_pool = ctx.enter_context(tc.tile_pool(name="turned", bufs=1))
        grouped_pool = ctx.enter_context(tc.tile_pool(name="grouped", bufs=3))
        next_mx_pool = ctx.enter_context(tc.tile_pool(name="next_mx", bufs=2))
        early_mx_pool = ctx.enter_context(tc.tile_pool(name="early_mx", bufs=len(BY_VECTOR)))
        result_pool = ctx.enter_context(tc.tile_pool(name="result", bufs=PAIRS))
        flipped_pool = ctx.enter_context(tc.psum_pool(name="flipped", bufs=4))
        acc_pool = ctx.enter_context(tc.psum_pool(name="acc", bufs=1))
        ctx.enter_context(tc.manual_schedule())

        raw = {}

        reordered = []

        def load_block(b):
            raw[b] = raw_pool.tile([P, CHUNKS * D8], BF16, name="block")
            if b in BY_VECTOR:
                for q4 in range(QUADRANTS):
                    partitions = slice(q4 * QUADRANT, (q4 + 1) * QUADRANT)
                    quarter = matrices[b][:, q4 * PIECE : (q4 + 1) * PIECE]
                    nc.gpsimd.dma_start(
                        out=raw[b][partitions, :].rearrange("r (m k) -> r m k", k=PIECE),
                        in_=quarter.rearrange("(m r) k -> r m k", r=QUADRANT),
                    )
                return
            if b not in (X, 0, 1):
                nc.sync.dma_start(
                    out=raw[b][:].rearrange("p (c k) -> p c k", k=D8),
                    in_=matrices[b].rearrange("(c p) k -> p c k", p=P),
                )
                return
            for c in range(CHUNKS):
                columns = slice(c * D8, (c + 1) * D8)
                chunk = x_halves[:, columns] if b == X else matrices[b][c * P : (c + 1) * P, :]
                nc.sync.dma_start(out=raw[b][:, columns], in_=chunk)

        def load_more():
            while len(raw) < len(load_order) and (
                len(raw) < BLOCKS_AHEAD or load_order[len(raw) - BLOCKS_AHEAD] in reordered
            ):
                load_block(load_order[len(raw)])

        load_more()

        identity = keep.tile([P, P], F32, name="identity")
        make_identity(nc, identity[:])

        warm = keep.tile([P, 1], F32, name="warm")
        nc.vector.memset(warm[:], 0.0)
        nc.scalar.activation(out=warm[:], in_=warm[:], func=mybir.ActivationFunctionType.Silu)

        zeros = keep.tile([P, F8], BF16, name="zeros")
        nc.vector.memset(zeros[:], 0.0)
        zero_sums = acc_pool.tile([P, F8], F32, name="acc%d" % (PAIRS - 1))

        def keep_warm(count):
            for turn in range(count):
                nc.tensor.matmul(
                    zero_sums[:], lhsT=zeros[:, :P], rhs=zeros[:], start=True, stop=True
                )

        keep_warm(WARM_START)

        ordered = {}

        def reorder(b, first, last, copy, dtype=BF16):
            if b not in ordered:
                ordered[b] = ordered_pool.tile(
                    [P, CHUNKS * D8], BF16, name="ordered", align_bytes=64
                )
            columns = slice(first * D8, last * D8)
            length = PIECE if b in BY_VECTOR else D8
            sizes = {
                "c": (last - first) * D8 // length,
                "s": SETS,
                "v": RUN_LENGTH if dtype == BF16 else RUN_LENGTH // 2,
            }
            out_view = ordered[b][:, columns].bitcast(dtype)
            in_view = raw[b][:, columns].bitcast(dtype)
            copy(
                out=out_view.rearrange("p (c s q v) -> p c s q v", **sizes),
                in_=in_view.rearrange("p (c q s v) -> p c s q v", **sizes),
            )
            if last == CHUNKS:
                reordered.append(b)
                load_more()

        def transpose_chunk(b, c):
            flipped = flipped_pool.tile([P, SETS, P], F32, name="flipped")
            for s in range(SETS):
                start = c * D8 + s * 2 * P
                pairs = ordered[b][:, start : start + 2 * P].bitcast(F32)
                nc.tensor.transpose(flipped[:, s, :], pairs, identity[:])
            return flipped

        x_signed = keep.tile([P, 2, PASSES, O, ROWS * PACK], BF16, name="x_signed", align_bytes=64)
        for l in range(CHUNKS):
            reorder(X, l, l + 1, nc.vector.tensor_copy)
        for l in range(CHUNKS):
            flipped = transpose_chunk(X, l)
            by_half = flipped[:].rearrange("p (g u) (r h) -> p h g r u", u=2, h=2)
            for h in range(2):
                words_out = x_signed[:, 0, :, 4 * h + l].bitcast(F32).rearrange(
                    "p g (r u) -> p g r u", u=2
                )
                if l % 2 == 0:
                    nc.vector.tensor_copy(out=words_out, in_=by_half[:, h])
                else:
                    nc.scalar.copy(out=words_out, in_=by_half[:, h])
            reorder(0, l, l + 1, nc.vector.tensor_copy)

        keep_warm(WARM_AFTER_X)

        x_codes = keep.tile([P, PASSES, len(slots) * ROWS], U32, name="x_codes", align_bytes=64)
        x_scales = keep.tile([P, PASSES, len(slots) * ROWS], U8, name="x_scales", align_bytes=64)
        filled = []

        def quantise_x_for(j):
            for pair in range(PAIRS):
                for slot in range(first_slot[(j, pair)], first_slot[(j, pair)] + 2):
                    if slot in filled:
                        continue
                    filled.append(slot)
                    i, sign = slots[slot]
                    columns = slice(slot * ROWS, (slot + 1) * ROWS)
                    for g in range(PASSES):
                        nc.vector.quantize_mx(
                            out=x_codes[:, g, columns].bitcast(FP8X4),
                            scales=x_scales[:, g, columns],
                            in_=x_signed[:, 0 if sign > 0 else 1, g, i, :],
                        )

        w_mx = {}

        def transpose_w(n):
            grouped = grouped_pool.tile([P, PASSES, F8 * PACK], BF16, name="grouped", align_bytes=64)
            grouped_words = grouped[:].bitcast(F32).rearrange("p g (o u) -> p g o u", u=2)
            for c in range(CHUNKS):
                flipped = transpose_chunk(n, c)
                nc.scalar.copy(
                    out=grouped_words[:, :, c * P : (c + 1) * P, :],
                    in_=flipped[:].rearrange("p (g u) o -> p g o u", u=2),
                )
            return grouped

        turned = {}

        def turn_on_vector(n, half):
            if half == 0:
                turned[n] = turned_pool.tile([P, CHUNKS * D8 // 2], F32, name="turned", align_bytes=64)
            columns = slice(half * D8, (half + 1) * D8)
            nc.vector.transpose(turned[n][:, columns], ordered[n][:].bitcast(F32)[:, columns])

        def group_turned(n):
            grouped = grouped_pool.tile([P, PASSES, F8 * PACK], BF16, name="grouped", align_bytes=64)
            by_pass = turned[n][:].rearrange(
                "p (m g u r) -> p g m r u", g=PASSES, u=2, r=QUADRANT
            )
            for g in range(PASSES):
                nc.scalar.copy(
                    out=grouped[:, g, :].bitcast(F32).rearrange(
                        "p (m r u) -> p m r u", r=QUADRANT, u=2
                    ),
                    in_=by_pass[:, g],
                )
            return grouped

        def quantise_w(n, grouped):
            w_mx_pool = early_mx_pool if n in BY_VECTOR else next_mx_pool
            codes = w_mx_pool.tile([P, PASSES, F8], U32, name="w_codes", align_bytes=64)
            scales = w_mx_pool.tile([P, PASSES, F8], U8, name="w_scales", align_bytes=64)
            nc.vector.quantize_mx(
                out=codes[:].rearrange("p g o -> p (g o)").bitcast(FP8X4),
                scales=scales[:].rearrange("p g o -> p (g o)"),
                in_=grouped[:].rearrange("p g c -> p (g c)"),
            )
            w_mx[n] = (codes, scales)

        acc = {}
        gate_act = {}

        def multiply(n):
            j = n % O
            codes, scales = w_mx[n]
            for pair in range(PAIRS):
                if j == 0:
                    acc[pair] = acc_pool.tile([P, F8], F32, name="acc%d" % pair)
                two_slots = slice(
                    first_slot[(j, pair)] * ROWS, (first_slot[(j, pair)] + 2) * ROWS
                )
                for g in range(PASSES):
                    nc.tensor.matmul_mx(
                        out=acc[pair][:],
                        lhsT=x_codes[:, g, two_slots].bitcast(FP8X4),
                        lhsT_scale=x_scales[:, g, two_slots],
                        rhs=codes[:, g, :].bitcast(FP8X4),
                        rhs_scale=scales[:, g, :],
                        start=(j == 0 and g == 0),
                        stop=(j == O - 1 and g == PASSES - 1),
                    )
                if n == O - 1:
                    gate_act[pair] = keep.tile([P, F8], F32, name="gate_act%d" % pair)
                    nc.scalar.activation(
                        out=gate_act[pair][:],
                        in_=acc[pair][:],
                        func=mybir.ActivationFunctionType.Silu,
                    )
                if n == 2 * O - 1:
                    result = result_pool.tile([P, F8], F32, name="result")
                    nc.vector.tensor_tensor(
                        out=result[:], in0=acc[pair][:], in1=gate_act[pair][:], op=mybir.AluOpType.mult
                    )
                    for half in range(2):
                        nc.sync.dma_start(
                            out=out_parts[2 * pair + half],
                            in_=result[half * ROWS : (half + 1) * ROWS, :],
                        )

        quantise_x_for(0)
        first_grouped = transpose_w(0)
        reorder(1, 0, 1, nc.vector.tensor_copy)
        quantise_w(0, first_grouped)
        keep_warm(WARM_AFTER_FIRST)
        for c in range(1, CHUNKS):
            reorder(1, c, c + 1, nc.scalar.copy, F32)
        nc.vector.tensor_scalar(
            out=x_signed[:, 1].rearrange("p g i c -> p (g i c)"),
            in0=x_signed[:, 0].rearrange("p g i c -> p (g i c)"),
            scalar1=-1.0,
            scalar2=None,
            op0=mybir.AluOpType.mult,
        )
        grouped = {}
        for n in range(2 * O):
            by_tensor = n + 1 not in BY_VECTOR and n + 1 < 2 * O
            for m in range(2 * O):
                if m not in BY_VECTOR and reorder_turn(m) == n:
                    reorder(m, 0, CHUNKS, nc.vector.tensor_copy)
            if n + 1 < O:
                quantise_x_for(n + 1)
            if by_tensor:
                grouped[n + 1] = transpose_w(n + 1)
            for m in BY_VECTOR:
                step = n - reorder_turn(m)
                if step == 0:
                    reorder(m, 0, CHUNKS, nc.vector.tensor_copy)
                if step in (1, 2):
                    turn_on_vector(m, step - 1)
                if step == 4:
                    quantise_w(m, grouped[m])
            if by_tensor:
                quantise_w(n + 1, grouped[n + 1])
            for m in BY_VECTOR:
                if n - reorder_turn(m) == 3:
                    grouped[m] = group_turned(m)
            multiply(n)
